import numpy as np
import ml_dtypes


def mxq(x, axis, fmt="e4m3"):
    dtype, down = {"e4m3": (ml_dtypes.float8_e4m3fn, 7), "e5m2": (ml_dtypes.float8_e5m2, 14)}[fmt]
    v = np.moveaxis(np.asarray(x, np.float32).astype(ml_dtypes.bfloat16).astype(np.float64), axis, -1)
    blocks = v.reshape(v.shape[:-1] + (-1, 32))
    amax = np.abs(blocks).max(-1, keepdims=True)
    byte = np.maximum(np.where(amax > 0, np.frexp(amax)[1] - 1 + 127, 0) - down, 1)
    scale = np.exp2(byte - 127.0)
    codes = (blocks / scale).astype(np.float32).astype(dtype).astype(np.float64)
    return np.moveaxis((codes * scale).reshape(v.shape), -1, axis)


WIDE = False


def mx_kscale(k):
    if not WIDE:
        return np.ones(k)
    levels = np.array([10, -10, 5, -5, 0])
    a = np.random.permutation(np.resize(levels, k // 512 * 4)).reshape(k // 512, 4)
    idx = np.arange(k)
    return np.exp2(a[idx // 512, idx % 128 // 32])


BF16 = ml_dtypes.bfloat16


def bf(x):
    return np.asarray(x, np.float32).astype(BF16)


def f64(x):
    return np.asarray(x).astype(np.float64)


B, S, D, R = 1, 1024, 1024, 4
GAMMA = 1.0


def setup_inputs():
    s = mx_kscale(D)
    p = np.random.standard_normal((R, D)) / np.sqrt(R * D)
    q = (np.random.standard_normal((B, S, R))[..., None] * p).sum(2) + np.random.standard_normal((B, S, D)) * 0.3 / np.sqrt(D)
    k = (np.random.standard_normal((B, S, R))[..., None] * p).sum(2) + np.random.standard_normal((B, S, D)) * 0.3 / np.sqrt(D)
    return {"q": bf(q), "k": bf(k), "x": bf(np.random.standard_normal((B, S, D)) * s),
            "Wv": bf(np.random.standard_normal((D, D)) * 0.125 * np.sqrt(S / D) / s[:, None]),
            "bv": bf(np.random.standard_normal(D) * 0.1)}


def reference(q, k, x, Wv, bv):
    q, k = f64(q), f64(k)
    v = (mxq(f64(x), 2, "e4m3") @ mxq(f64(Wv), 0, "e4m3")) + f64(bv)
    q_sq = np.sum(q * q, axis=-1)
    k_sq = np.sum(k * k, axis=-1)
    qk = mxq(q, 2, "e4m3") @ mxq(k.transpose(0, 2, 1), 1, "e4m3")
    dist_sq = q_sq[:, :, None] + k_sq[:, None, :] - 2.0 * qk
    scores = np.exp(-GAMMA * dist_sq)
    e = np.exp(scores - scores.max(-1, keepdims=True))
    return (mxq(e, 2, "e4m3") @ mxq(v, 1, "e4m3")) / e.sum(-1, keepdims=True)

@@ -1,0 +1,390 @@
+from contextlib import ExitStack
+
+import concourse.mybir as mybir
+from concourse.masks import make_identity
+
+F32 = mybir.dt.float32
+BF16 = mybir.dt.bfloat16
+U32 = mybir.dt.uint32
+U8 = mybir.dt.uint8
+FP8X4 = mybir.dt.float8_e4m3fn_x4
+ALU = mybir.AluOpType
+ACT = mybir.ActivationFunctionType
+AX = mybir.AxisListType
+
+P = 128
+S = 1024
+D = 1024
+TILES = S // P
+PACK = 4
+K_PASS = P * PACK
+PASSES = D // K_PASS
+BANK = 512
+HALVES = S // BANK
+FLOPS = 3 * 2 * S * D * D
+
+
+def tile_selfattentionhybrid_pa_kernel(tc, q, k, x, Wv, bv, out):
+    nc = tc.nc
+    with ExitStack() as ctx:
+        ctx.enter_context(tc.manual_schedule())
+        const = ctx.enter_context(tc.tile_pool(name="const", bufs=1))
+        raws = ctx.enter_context(tc.tile_pool(name="raws", bufs=1))
+        keep = ctx.enter_context(tc.tile_pool(name="keep", bufs=1))
+        grp = ctx.enter_context(tc.tile_pool(name="grp", bufs=2))
+        work = ctx.enter_context(tc.tile_pool(name="work", bufs=3))
+        small = ctx.enter_context(tc.tile_pool(name="small", bufs=4))
+        psum = ctx.enter_context(tc.psum_pool(name="psum", bufs=8))
+
+        raw = {}
+        for name in ("k", "q", "x", "w"):
+            raw[name] = raws.tile([P, TILES * D], BF16, name="raw_" + name)
+        rows = {
+            "k": k.flatten_outer_dims().rearrange("(g p t) f -> p g (t f)", g=PASSES, p=P, t=PACK),
+            "x": x.flatten_outer_dims().rearrange("(g p t) f -> p g (t f)", g=PASSES, p=P, t=PACK),
+            "q": q.flatten_outer_dims().rearrange("(p g t) f -> p g (t f)", g=PASSES, p=P, t=PACK),
+        }
+        out_rows = out.flatten_outer_dims().rearrange("(p c) d -> p c d", p=P)
+        w_rows = Wv.rearrange("(b p e) d -> p b (e d)", b=2 * PASSES, p=P, e=2)
+
+        warm = const.tile([P, 8], F32, name="warm")
+        ident_f = const.tile([P, P], F32, name="ident_f")
+        ident_b = const.tile([P, P], BF16, name="ident_b")
+        ones_b = const.tile([P, P], BF16, name="ones_b")
+        bias_row = const.tile([P, D], BF16, name="bias_row")
+        bias_all = const.tile([P, D], BF16, name="bias_all")
+        ksq_all = const.tile([P, S], F32, name="ksq_all")
+        ksq = const.tile([P, TILES, 8], F32, name="ksq")
+        qsq = const.tile([P, TILES, 8], F32, name="qsq")
+        neg_qsq = const.tile([P, TILES, 8], F32, name="neg_qsq")
+        words = {}
+        scales = {}
+        for name in ("k", "q", "x", "w", "v", "e"):
+            words[name] = keep.tile([P, PASSES, S], U32, name="words_" + name, align_bytes=64)
+            scales[name] = keep.tile([P, PASSES, S], U8, name="scales_" + name, align_bytes=64)
+        e_words = words["e"][:].rearrange("p a (b n) -> p (a b) n", n=PASSES * P)
+        e_scales = scales["e"][:].rearrange("p a (b n) -> p (a b) n", n=PASSES * P)
+        live = {}
+
+        def bank_tile(key, shape, dtype):
+            live[key] = psum.tile(shape, dtype, name="bank", tag="bank")
+            return live[key]
+
+        def copy_on(engine, dst, src):
+            if engine == "vector":
+                nc.vector.tensor_copy(out=dst, in_=src)
+            else:
+                nc.scalar.copy(out=dst, in_=src)
+
+        def mx_pass(acc, a_words, a_scales, b_words, b_scales, first, last):
+            nc.tensor.matmul_mx(out=acc, lhsT=a_words.bitcast(FP8X4), lhsT_scale=a_scales, rhs=b_words.bitcast(FP8X4),
+                                rhs_scale=b_scales, start=first, stop=last)
+
+        def mx_group(acc, a, a_cols, b, b_cols):
+            for g in range(PASSES):
+                mx_pass(acc, words[a][:, g, a_cols], scales[a][:, g, a_cols], words[b][:, g, b_cols],
+                        scales[b][:, g, b_cols], g == 0, g == PASSES - 1)
+
+        def quantise(name, g, cols, src):
+            nc.vector.quantize_mx(out=words[name][:, g, cols].bitcast(FP8X4), scales=scales[name][:, g, cols], in_=src)
+
+        def constants():
+            nc.vector.memset(warm[:], 0.0)
+            nc.scalar.activation(out=warm[:], in_=warm[:], func=ACT.Exp)
+            make_identity(nc, ident_f[:])
+            nc.gpsimd.memset(bias_row[:], 0.0)
+            nc.gpsimd.dma_start(out=bias_row[0:1, :], in_=bv.unsqueeze(0))
+            nc.gpsimd.memset(ones_b[:], 1.0)
+            make_identity(nc, ident_b[:])
+
+        def load_rows(name, c, n):
+            t = c % PACK
+            nc.sync.dma_start(out=raw[name][:, D * c : D * (c + n)], in_=rows[name][:, c // PACK, D * t : D * (t + n)])
+
+        def load_w(g):
+            nc.sync.dma_start(out=raw["w"][:, PACK * D * g : PACK * D * (g + 1)].rearrange("p (b n) -> p b n", b=2),
+                              in_=w_rows[:, 2 * g : 2 * g + 2, :])
+
+        def turn_rows(name, c):
+            pairs = raw[name][:, D * c : D * (c + 1)].bitcast(F32)
+            bank = bank_tile(("turned", name, c), [P, 2 * PASSES, P], F32)
+            for b in range(2 * PASSES):
+                nc.tensor.transpose(bank[:, b, :], pairs[:, P * b : P * (b + 1)], ident_f[:])
+
+        def copy_words(name, c, engine):
+            half, cc = c // PACK, c % PACK
+            if ("grouped", name, half) not in live:
+                live[("grouped", name, half)] = grp.tile([P, PASSES * PACK * BANK], BF16, name="grp_" + name, tag="grp_t",
+                                                         align_bytes=64)
+            dst = live[("grouped", name, half)][:].bitcast(F32).rearrange("p (g c r u) -> p g c r u", g=PASSES, c=PACK, u=2)
+            copy_on(engine, dst[:, :, cc, :, :], live[("turned", name, c)][:].rearrange("p (g u) r -> p g r u", u=2))
+
+        def quantise_rows(name, half, g):
+            quantise(name, g, slice(BANK * half, BANK * (half + 1)),
+                     live[("grouped", name, half)][:, PACK * BANK * g : PACK * BANK * (g + 1)])
+
+        def square_rows(name, c):
+            unused = work.tile([P, D], BF16, name="unused", bufs=1)
+            dst = ksq if name == "k" else qsq
+            nc.scalar.activation(out=unused[:], in_=raw[name][:, D * c : D * (c + 1)], func=ACT.Square,
+                                 accum_out=dst[:, c, 0:1])
+            if name == "q":
+                nc.gpsimd.tensor_scalar(out=neg_qsq[:, c, 0:1], in0=qsq[:, c, 0:1], scalar1=-1.0, scalar2=0.0,
+                                        op0=ALU.mult, op1=ALU.add)
+
+        def spread_ksq(half):
+            bank = bank_tile(("ksq", half), [P, PACK, P], F32)
+            for t in range(PACK):
+                nc.tensor.matmul(out=bank[:, t, :], lhsT=ksq[:, PACK * half + t, 0:1].to_broadcast([P, P]), rhs=ident_f[:],
+                                 start=True, stop=True)
+
+        def copy_ksq(half):
+            nc.scalar.copy(out=ksq_all[:, BANK * half : BANK * (half + 1)], in_=live[("ksq", half)][:].rearrange("p t r -> p (t r)"))
+
+        def spread_bias(half):
+            bank = bank_tile(("bias", half), [P, BANK], F32)
+            nc.tensor.matmul(out=bank[:], lhsT=ones_b[:], rhs=bias_row[:, BANK * half : BANK * (half + 1)], start=True, stop=True)
+
+        def copy_bias(half):
+            nc.scalar.copy(out=bias_all[:, BANK * half : BANK * (half + 1)], in_=live[("bias", half)][:])
+
+        def regroup_w(g, half):
+            live[("w", g, half)] = grp.tile([P, PACK * BANK], BF16, name="grp_w", align_bytes=64)
+            src = raw["w"][:, PACK * D * g : PACK * D * (g + 1)].rearrange("p (t d) -> p t d", t=PACK)
+            nc.vector.tensor_copy(out=live[("w", g, half)][:].rearrange("p (c i t) -> p c t i", i=4, t=PACK),
+                                  in_=src[:, :, BANK * half : BANK * (half + 1)].rearrange("p t (c i) -> p c t i", i=4))
+
+        def quantise_w(g, half):
+            quantise("w", g, slice(BANK * half, BANK * (half + 1)), live[("w", g, half)][:])
+
+        def v_matmuls(n):
+            kp, cols = n // 8, slice(P * (n % 8), P * (n % 8 + 1))
+            bank = bank_tile(("v", n), [P, PACK, P], F32)
+            for t in range(PACK):
+                c = PACK * kp + t
+                mx_group(bank[:, t, :], "x", slice(P * c, P * (c + 1)), "w", cols)
+
+        def v_bias(n):
+            group, cols = n // 4, slice(P * (n % 8), P * (n % 8 + 1))
+            if ("v_grouped", group) not in live:
+                live[("v_grouped", group)] = grp.tile([P, PACK * BANK], BF16, name="grp_v", align_bytes=64)
+            nc.vector.tensor_tensor(
+                out=live[("v_grouped", group)][:, BANK * (n % 4) : BANK * (n % 4 + 1)].rearrange("p (d t) -> p d t", t=PACK),
+                in0=live[("v", n)][:].rearrange("p t d -> p d t"),
+                in1=bias_all[:, cols].unsqueeze(2).to_broadcast([P, P, PACK]),
+                op=ALU.add,
+            )
+
+        def quantise_v(group):
+            quantise("v", group // 2, slice(BANK * (group % 2), BANK * (group % 2 + 1)), live[("v_grouped", group)][:])
+
+        def score_matmuls(c):
+            for h in range(HALVES):
+                mx_group(bank_tile(("qk", c, h), [P, BANK], F32)[:], "q", slice(P * c, P * (c + 1)), "k",
+                         slice(BANK * h, BANK * (h + 1)))
+
+        def distance(c):
+            live[("scores", c)] = work.tile([P, S], F32, name="scores")
+            for h in range(HALVES):
+                cols = slice(BANK * h, BANK * (h + 1))
+                nc.vector.scalar_tensor_tensor(out=live[("scores", c)][:, cols], in0=live[("qk", c, h)][:], scalar=-2.0,
+                                               in1=ksq_all[:, cols], op0=ALU.mult, op1=ALU.add)
+
+        def first_exp(c):
+            sc = live[("scores", c)]
+            nc.scalar.activation(out=sc[:], in_=sc[:], func=ACT.Exp, bias=neg_qsq[:, c, 0:1], scale=-1.0)
+
+        def row_max(c):
+            live[("neg_max", c)] = small.tile([P, 1], F32, name="neg_max")
+            nc.vector.tensor_reduce(out=live[("neg_max", c)][:], in_=live[("scores", c)][:], axis=AX.X, op=ALU.max, negate=True)
+
+        def second_exp(c):
+            live[("e", c)] = work.tile([P, S], BF16, name="e")
+            live[("row_sum", c)] = small.tile([P, 1], F32, name="row_sum")
+            nc.scalar.activation(out=live[("e", c)][:], in_=live[("scores", c)][:], func=ACT.Exp, bias=live[("neg_max", c)][:],
+                                 scale=1.0, accum_out=live[("row_sum", c)][:])
+
+        def turn_e(c, banks):
+            planes = TILES // banks
+            for i in range(banks):
+                bank = bank_tile(("e_turned", c, i), [P, planes, P], BF16)
+                for j in range(planes):
+                    b = planes * i + j
+                    nc.tensor.transpose(bank[:, j, :], live[("e", c)][:, P * b : P * (b + 1)], ident_b[:])
+
+        def copy_e(c, engine, banks, i):
+            if ("e_grouped", c) not in live:
+                live[("e_grouped", c)] = grp.tile([P, S], BF16, name="grp_e", align_bytes=64)
+            width = S // banks
+            copy_on(engine, live[("e_grouped", c)][:, width * i : width * (i + 1)].rearrange("p (g r t) -> p g r t", r=P, t=PACK),
+                    live[("e_turned", c, i)][:].rearrange("p (g t) r -> p g r t", t=PACK))
+
+        def quantise_e(c):
+            nc.vector.quantize_mx(out=e_words[:, c, :].bitcast(FP8X4), scales=e_scales[:, c, :], in_=live[("e_grouped", c)][:])
+            live[("inv_sum", c)] = small.tile([P, 1], F32, name="inv_sum", bufs=8)
+            nc.vector.reciprocal(out=live[("inv_sum", c)][:], in_=live[("row_sum", c)][:])
+
+        def out_matmuls(c):
+            for h in range(HALVES):
+                bank = bank_tile(("out", c, h), [P, BANK], F32)
+                cols = slice(BANK * h, BANK * (h + 1))
+                for kp in range(PASSES):
+                    mx_pass(bank[:], e_words[:, c, P * kp : P * (kp + 1)], e_scales[:, c, P * kp : P * (kp + 1)],
+                            words["v"][:, kp, cols], scales["v"][:, kp, cols], kp == 0, kp == PASSES - 1)
+
+        def out_copy(c, h, engine):
+            if ("result", c) not in live:
+                live[("result", c)] = work.tile([P, D], F32, name="result")
+            dst = live[("result", c)][:, BANK * h : BANK * (h + 1)]
+            if engine == "vector":
+                nc.vector.tensor_scalar_mul(out=dst, in0=live[("out", c, h)][:], scalar1=live[("inv_sum", c)][:])
+            else:
+                nc.scalar.activation(out=dst, in_=live[("out", c, h)][:], func=ACT.Copy, scale=live[("inv_sum", c)][:])
+            nc.sync.dma_start(out=out_rows[:, c, BANK * h : BANK * (h + 1)], in_=dst)
+
+        constants()
+        load_rows("k", 0, 1)
+        load_rows("k", 1, 1)
+        for c in (2, 4, 6):
+            load_rows("k", c, 2)
+        load_w(0)
+        load_rows("x", 0, 2)
+        load_rows("x", 2, 2)
+        load_w(1)
+        load_rows("x", 4, 2)
+        load_rows("x", 6, 2)
+        for c in (0, 2, 4, 6):
+            load_rows("q", c, 2)
+
+        for c in range(TILES):
+            turn_rows("k", c)
+        for c in range(5):
+            copy_words("k", c, "vector")
+        quantise_rows("k", 0, 0)
+        copy_words("k", 5, "vector")
+        quantise_rows("k", 0, 1)
+        copy_words("k", 6, "vector")
+        copy_words("k", 7, "vector")
+        quantise_rows("k", 1, 0)
+        quantise_rows("k", 1, 1)
+        for g in range(PASSES):
+            regroup_w(g, 0)
+            regroup_w(g, 1)
+            quantise_w(g, 0)
+            quantise_w(g, 1)
+        for c in range(TILES):
+            square_rows("k", c)
+        spread_ksq(0)
+        for c in range(4):
+            turn_rows("x", c)
+        spread_ksq(1)
+        spread_bias(0)
+        spread_bias(1)
+        for c in range(4, TILES):
+            turn_rows("x", c)
+        for c in range(4):
+            turn_rows("q", c)
+        for c in range(4):
+            copy_words("x", c, "scalar")
+        copy_ksq(0)
+        copy_ksq(1)
+        for c in range(4, TILES):
+            copy_words("x", c, "scalar")
+        copy_bias(0)
+        copy_bias(1)
+        copy_words("q", 0, "scalar")
+        copy_words("q", 1, "scalar")
+        square_rows("q", 0)
+        copy_words("q", 2, "scalar")
+        copy_words("q", 3, "scalar")
+        square_rows("q", 1)
+        square_rows("q", 2)
+        for half in range(2):
+            for g in range(PASSES):
+                quantise_rows("x", half, g)
+
+        v_steps = []
+        for n in range(16):
+            v_steps.append(("block", n))
+            if n % 4 == 0 and n > 0:
+                v_steps.append(("words", n // 4 - 1))
+        v_steps.append(("words", 3))
+        made = [0]
+
+        def v_tensor(count):
+            for n in range(made[0], min(made[0] + count, 16)):
+                v_matmuls(n)
+            made[0] = min(made[0] + count, 16)
+
+        def v_vector(blocks):
+            while v_steps and (blocks > 0 or len(v_steps) == 1):
+                kind, n = v_steps.pop(0)
+                if kind == "block":
+                    v_bias(n)
+                    blocks -= 1
+                else:
+                    quantise_v(n)
+
+        v_tensor(5 + 2)
+        v_vector(5)
+        quantise_rows("q", 0, 0)
+        quantise_rows("q", 0, 1)
+        score_matmuls(0)
+        score_matmuls(1)
+        distance(0)
+
+        V_BLOCKS = (3, 3, 3, 2)
+        V_DONE = len(V_BLOCKS)
+        OUT_LAG = 3
+        for p in range(TILES):
+            due = [c for c in range(TILES) if max(c + OUT_LAG, V_DONE) == p]
+            blocks = V_BLOCKS[p] if p < V_DONE else 0
+            for c in due:
+                out_matmuls(c)
+            if p == 0:
+                for c in range(4, TILES):
+                    turn_rows("q", c)
+            if p + 2 < TILES:
+                score_matmuls(p + 2)
+            v_tensor(blocks)
+            if p + 1 < TILES:
+                distance(p + 1)
+            first_exp(p)
+            row_max(p)
+            if p >= 1:
+                second_exp(p - 1)
+                turn_e(p - 1, 1)
+            if p == 0:
+                for c in range(4, TILES):
+                    copy_words("q", c, "scalar")
+            elif p + 2 < TILES:
+                square_rows("q", p + 2)
+            if p >= 2:
+                copy_e(p - 2, "scalar", 1, 0)
+            if p == 1:
+                quantise_rows("q", 1, 0)
+                quantise_rows("q", 1, 1)
+            v_vector(blocks)
+            for c in due:
+                out_copy(c, 0, "vector")
+                out_copy(c, 1, "vector")
+            if p >= 2:
+                quantise_e(p - 2)
+
+        last = TILES - 1
+        second_exp(last)
+        turn_e(last, 2)
+        out_matmuls(5)
+        copy_e(6, "vector", 1, 0)
+        quantise_e(6)
+        out_matmuls(6)
+        out_copy(5, 0, "scalar")
+        copy_e(last, "scalar", 2, 1)
+        copy_e(last, "vector", 2, 0)
+        quantise_e(last)
+        out_matmuls(last)
+        out_copy(5, 1, "scalar")
+        out_copy(6, 1, "scalar")
+        out_copy(6, 0, "vector")
+        out_copy(last, 0, "vector")
+        out_copy(last, 1, "scalar")

@@ -40,23 +40,22 @@ def tile_selfattentionhybrid_pa_kernel(tc, q, k, x, Wv, bv, out):
         for name in ("k", "q", "x", "w"):
             raw[name] = raws.tile([P, TILES * D], BF16, name="raw_" + name)
         rows = {
-            "k": k.flatten_outer_dims().rearrange("(g p t) f -> p g (t f)", g=PASSES, p=P, t=PACK),
-            "x": x.flatten_outer_dims().rearrange("(g p t) f -> p g (t f)", g=PASSES, p=P, t=PACK),
-            "q": q.flatten_outer_dims().rearrange("(p g t) f -> p g (t f)", g=PASSES, p=P, t=PACK),
+            "k": k.flatten_outer_dims().rearrange("(c p) f -> p c f", p=P),
+            "x": x.flatten_outer_dims().rearrange("(b p e) f -> p b (e f)", p=P, e=2),
+            "q": q.flatten_outer_dims().rearrange("(p b e) f -> p b (e f)", p=P, e=2),
         }
         out_rows = out.flatten_outer_dims().rearrange("(p c) d -> p c d", p=P)
         w_rows = Wv.rearrange("(b p e) d -> p b (e d)", b=2 * PASSES, p=P, e=2)
 
         warm = const.tile([P, 8], F32, name="warm")
         ident_f = const.tile([P, P], F32, name="ident_f")
-        ident_b = const.tile([P, P], BF16, name="ident_b")
         ones_b = const.tile([P, P], BF16, name="ones_b")
+        ones_f = const.tile([P, P], F32, name="ones_f")
+        minus_one = const.tile([P, 1], F32, name="minus_one")
         bias_row = const.tile([P, D], BF16, name="bias_row")
         bias_all = const.tile([P, D], BF16, name="bias_all")
         ksq_all = const.tile([P, S], F32, name="ksq_all")
-        ksq = const.tile([P, TILES, 8], F32, name="ksq")
-        qsq = const.tile([P, TILES, 8], F32, name="qsq")
-        neg_qsq = const.tile([P, TILES, 8], F32, name="neg_qsq")
+        neg_qsq = const.tile([P, TILES * 8], F32, name="neg_qsq")
         words = {}
         scales = {}
         for name in ("k", "q", "x", "w", "v", "e"):
@@ -95,11 +94,15 @@ def tile_selfattentionhybrid_pa_kernel(tc, q, k, x, Wv, bv, out):
             nc.gpsimd.memset(bias_row[:], 0.0)
             nc.gpsimd.dma_start(out=bias_row[0:1, :], in_=bv.unsqueeze(0))
             nc.gpsimd.memset(ones_b[:], 1.0)
-            make_identity(nc, ident_b[:])
+            nc.gpsimd.memset(ones_f[:], 1.0)
+            nc.gpsimd.memset(minus_one[:], -1.0)
 
         def load_rows(name, c, n):
-            t = c % PACK
-            nc.sync.dma_start(out=raw[name][:, D * c : D * (c + n)], in_=rows[name][:, c // PACK, D * t : D * (t + n)])
+            dst = raw[name][:, D * c : D * (c + n)]
+            if name == "k":
+                nc.sync.dma_start(out=dst.rearrange("p (c f) -> p c f", f=D), in_=rows[name][:, c : c + n, :])
+            else:
+                nc.sync.dma_start(out=dst, in_=rows[name][:, c // 2, :])
 
         def load_w(g):
             nc.sync.dma_start(out=raw["w"][:, PACK * D * g : PACK * D * (g + 1)].rearrange("p (b n) -> p b n", b=2),
@@ -115,7 +118,7 @@ def tile_selfattentionhybrid_pa_kernel(tc, q, k, x, Wv, bv, out):
             half, cc = c // PACK, c % PACK
             if ("grouped", name, half) not in live:
                 live[("grouped", name, half)] = grp.tile([P, PASSES * PACK * BANK], BF16, name="grp_" + name, tag="grp_t",
-                                                         align_bytes=64)
+                                                         bufs=3, align_bytes=64)
             dst = live[("grouped", name, half)][:].bitcast(F32).rearrange("p (g c r u) -> p g c r u", g=PASSES, c=PACK, u=2)
             copy_on(engine, dst[:, :, cc, :, :], live[("turned", name, c)][:].rearrange("p (g u) r -> p g r u", u=2))
 
@@ -123,23 +126,45 @@ def tile_selfattentionhybrid_pa_kernel(tc, q, k, x, Wv, bv, out):
             quantise(name, g, slice(BANK * half, BANK * (half + 1)),
                      live[("grouped", name, half)][:, PACK * BANK * g : PACK * BANK * (g + 1)])
 
-        def square_rows(name, c):
+        def square_q(c):
             unused = work.tile([P, D], BF16, name="unused", bufs=1)
-            dst = ksq if name == "k" else qsq
-            nc.scalar.activation(out=unused[:], in_=raw[name][:, D * c : D * (c + 1)], func=ACT.Square,
-                                 accum_out=dst[:, c, 0:1])
-            if name == "q":
-                nc.gpsimd.tensor_scalar(out=neg_qsq[:, c, 0:1], in0=qsq[:, c, 0:1], scalar1=-1.0, scalar2=0.0,
-                                        op0=ALU.mult, op1=ALU.add)
+            qsq = small.tile([P, 1], F32, name="qsq")
+            nc.scalar.activation(out=unused[:], in_=raw["q"][:, D * c : D * (c + 1)], func=ACT.Square, accum_out=qsq[:])
+            nc.gpsimd.tensor_scalar(out=neg_qsq[:, 8 * c : 8 * c + 1], in0=qsq[:], scalar1=-1.0, scalar2=0.0, op0=ALU.mult, op1=ALU.add)
+
+        def gram(name, c):
+            half, cc = c // PACK, c % PACK
+            if cc == 0:
+                bank_tile(("gram", name, half), [P, PACK, P], F32)
+            bank = live[("gram", name, half)]
+            features = live[("grouped", name, half)][:].rearrange("p (g c r t) -> p g c r t", g=PASSES, c=PACK, t=PACK)
+            for g in range(PASSES):
+                for t in range(PACK):
+                    operand = features[:, g, cc, :, t]
+                    nc.tensor.matmul(out=bank[:, cc, :], lhsT=operand, rhs=operand, start=g == 0 and t == 0,
+                                     stop=g == PASSES - 1 and t == PACK - 1)
+
+        def keep_diagonal(name, half):
+            live[("diagonal", name, half)] = work.tile([P, PACK, P], F32, name="diagonal", bufs=2)
+            nc.vector.tensor_tensor(out=live[("diagonal", name, half)][:], in0=live[("gram", name, half)][:],
+                                    in1=ident_f[:].unsqueeze(1).to_broadcast([P, PACK, P]), op=ALU.mult)
 
         def spread_ksq(half):
-            bank = bank_tile(("ksq", half), [P, PACK, P], F32)
+            bank = bank_tile(("ksq", half), [P, BANK], F32)
+            nc.tensor.matmul(out=bank[:], lhsT=ones_f[:], rhs=live[("diagonal", "k", half)][:].rearrange("p t r -> p (t r)"),
+                             start=True, stop=True)
+
+        def turn_qsq(half):
+            bank = bank_tile(("qsq", half), [P, PACK], F32)
             for t in range(PACK):
-                nc.tensor.matmul(out=bank[:, t, :], lhsT=ksq[:, PACK * half + t, 0:1].to_broadcast([P, P]), rhs=ident_f[:],
+                nc.tensor.matmul(out=bank[:, t : t + 1], lhsT=live[("diagonal", "q", half)][:, t, :], rhs=minus_one[:],
                                  start=True, stop=True)
 
+        def copy_qsq(half):
+            nc.scalar.copy(out=neg_qsq[:, 8 * PACK * half : 8 * PACK * (half + 1) : 8], in_=live[("qsq", half)][:])
+
         def copy_ksq(half):
-            nc.scalar.copy(out=ksq_all[:, BANK * half : BANK * (half + 1)], in_=live[("ksq", half)][:].rearrange("p t r -> p (t r)"))
+            nc.scalar.copy(out=ksq_all[:, BANK * half : BANK * (half + 1)], in_=live[("ksq", half)][:])
 
         def spread_bias(half):
             bank = bank_tile(("bias", half), [P, BANK], F32)
@@ -148,24 +173,29 @@ def tile_selfattentionhybrid_pa_kernel(tc, q, k, x, Wv, bv, out):
         def copy_bias(half):
             nc.scalar.copy(out=bias_all[:, BANK * half : BANK * (half + 1)], in_=live[("bias", half)][:])
 
-        def regroup_w(g, half):
+        def regroup_w(g, half, engine):
             live[("w", g, half)] = grp.tile([P, PACK * BANK], BF16, name="grp_w", align_bytes=64)
             src = raw["w"][:, PACK * D * g : PACK * D * (g + 1)].rearrange("p (t d) -> p t d", t=PACK)
-            nc.vector.tensor_copy(out=live[("w", g, half)][:].rearrange("p (c i t) -> p c t i", i=4, t=PACK),
-                                  in_=src[:, :, BANK * half : BANK * (half + 1)].rearrange("p t (c i) -> p c t i", i=4))
+            copy_on(engine, live[("w", g, half)][:].rearrange("p (c i t) -> p c t i", i=4, t=PACK),
+                    src[:, :, BANK * half : BANK * (half + 1)].rearrange("p t (c i) -> p c t i", i=4))
 
         def quantise_w(g, half):
             quantise("w", g, slice(BANK * half, BANK * (half + 1)), live[("w", g, half)][:])
 
+        def v_place(n):
+            c = 4 * (n // 8) + n % 4
+            return (n // 4) % 2, slice(P * c, P * (c + 1))
+
         def v_matmuls(n):
-            kp, cols = n // 8, slice(P * (n % 8), P * (n % 8 + 1))
+            kp, cols = v_place(n)
             bank = bank_tile(("v", n), [P, PACK, P], F32)
             for t in range(PACK):
                 c = PACK * kp + t
                 mx_group(bank[:, t, :], "x", slice(P * c, P * (c + 1)), "w", cols)
 
         def v_bias(n):
-            group, cols = n // 4, slice(P * (n % 8), P * (n % 8 + 1))
+            group = n // 4
+            kp, cols = v_place(n)
             if ("v_grouped", group) not in live:
                 live[("v_grouped", group)] = grp.tile([P, PACK * BANK], BF16, name="grp_v", align_bytes=64)
             nc.vector.tensor_tensor(
@@ -176,23 +206,22 @@ def tile_selfattentionhybrid_pa_kernel(tc, q, k, x, Wv, bv, out):
             )
 
         def quantise_v(group):
-            quantise("v", group // 2, slice(BANK * (group % 2), BANK * (group % 2 + 1)), live[("v_grouped", group)][:])
+            quantise("v", group % 2, slice(BANK * (group // 2), BANK * (group // 2 + 1)), live[("v_grouped", group)][:])
 
-        def score_matmuls(c):
-            for h in range(HALVES):
-                mx_group(bank_tile(("qk", c, h), [P, BANK], F32)[:], "q", slice(P * c, P * (c + 1)), "k",
-                         slice(BANK * h, BANK * (h + 1)))
+        def score_matmuls(c, h):
+            mx_group(bank_tile(("qk", c, h), [P, BANK], F32)[:], "q", slice(P * c, P * (c + 1)), "k",
+                     slice(BANK * h, BANK * (h + 1)))
 
-        def distance(c):
-            live[("scores", c)] = work.tile([P, S], F32, name="scores")
-            for h in range(HALVES):
-                cols = slice(BANK * h, BANK * (h + 1))
-                nc.vector.scalar_tensor_tensor(out=live[("scores", c)][:, cols], in0=live[("qk", c, h)][:], scalar=-2.0,
-                                               in1=ksq_all[:, cols], op0=ALU.mult, op1=ALU.add)
+        def distance(c, h):
+            if h == 0:
+                live[("scores", c)] = work.tile([P, S], F32, name="scores", bufs=5)
+            cols = slice(BANK * h, BANK * (h + 1))
+            nc.vector.scalar_tensor_tensor(out=live[("scores", c)][:, cols], in0=live[("qk", c, h)][:], scalar=-2.0,
+                                           in1=ksq_all[:, cols], op0=ALU.mult, op1=ALU.add)
 
         def first_exp(c):
             sc = live[("scores", c)]
-            nc.scalar.activation(out=sc[:], in_=sc[:], func=ACT.Exp, bias=neg_qsq[:, c, 0:1], scale=-1.0)
+            nc.scalar.activation(out=sc[:], in_=sc[:], func=ACT.Exp, bias=neg_qsq[:, 8 * c : 8 * c + 1], scale=-1.0)
 
         def row_max(c):
             live[("neg_max", c)] = small.tile([P, 1], F32, name="neg_max")
@@ -205,37 +234,36 @@ def tile_selfattentionhybrid_pa_kernel(tc, q, k, x, Wv, bv, out):
                                  scale=1.0, accum_out=live[("row_sum", c)][:])
 
         def turn_e(c, banks):
-            planes = TILES // banks
+            pairs = live[("e", c)][:].bitcast(F32)
+            planes = 2 * PASSES // banks
             for i in range(banks):
-                bank = bank_tile(("e_turned", c, i), [P, planes, P], BF16)
+                bank = bank_tile(("e_turned", c, i), [P, planes, P], F32)
                 for j in range(planes):
                     b = planes * i + j
-                    nc.tensor.transpose(bank[:, j, :], live[("e", c)][:, P * b : P * (b + 1)], ident_b[:])
+                    nc.tensor.transpose(bank[:, j, :], pairs[:, P * b : P * (b + 1)], ident_f[:])
 
         def copy_e(c, engine, banks, i):
             if ("e_grouped", c) not in live:
-                live[("e_grouped", c)] = grp.tile([P, S], BF16, name="grp_e", align_bytes=64)
+                live[("e_grouped", c)] = grp.tile([P, S], BF16, name="grp_e", bufs=3, align_bytes=64)
             width = S // banks
-            copy_on(engine, live[("e_grouped", c)][:, width * i : width * (i + 1)].rearrange("p (g r t) -> p g r t", r=P, t=PACK),
-                    live[("e_turned", c, i)][:].rearrange("p (g t) r -> p g r t", t=PACK))
+            copy_on(engine, live[("e_grouped", c)][:, width * i : width * (i + 1)].bitcast(F32).rearrange("p (g r u) -> p g r u", r=P, u=2),
+                    live[("e_turned", c, i)][:].rearrange("p (g u) r -> p g r u", u=2))
 
         def quantise_e(c):
             nc.vector.quantize_mx(out=e_words[:, c, :].bitcast(FP8X4), scales=e_scales[:, c, :], in_=live[("e_grouped", c)][:])
             live[("inv_sum", c)] = small.tile([P, 1], F32, name="inv_sum", bufs=8)
             nc.vector.reciprocal(out=live[("inv_sum", c)][:], in_=live[("row_sum", c)][:])
 
-        def out_matmuls(c):
-            for h in range(HALVES):
-                bank = bank_tile(("out", c, h), [P, BANK], F32)
-                cols = slice(BANK * h, BANK * (h + 1))
-                for kp in range(PASSES):
-                    mx_pass(bank[:], e_words[:, c, P * kp : P * (kp + 1)], e_scales[:, c, P * kp : P * (kp + 1)],
-                            words["v"][:, kp, cols], scales["v"][:, kp, cols], kp == 0, kp == PASSES - 1)
+        def out_matmuls(c, h):
+            bank = bank_tile(("out", c, h), [P, BANK], F32)
+            cols = slice(BANK * h, BANK * (h + 1))
+            for kp in range(PASSES):
+                mx_pass(bank[:], e_words[:, c, P * kp : P * (kp + 1)], e_scales[:, c, P * kp : P * (kp + 1)],
+                        words["v"][:, kp, cols], scales["v"][:, kp, cols], kp == 0, kp == PASSES - 1)
 
         def out_copy(c, h, engine):
-            if ("result", c) not in live:
-                live[("result", c)] = work.tile([P, D], F32, name="result")
-            dst = live[("result", c)][:, BANK * h : BANK * (h + 1)]
+            result = work.tile([P, BANK], F32, name="result", bufs=10)
+            dst = result[:]
             if engine == "vector":
                 nc.vector.tensor_scalar_mul(out=dst, in0=live[("out", c, h)][:], scalar1=live[("inv_sum", c)][:])
             else:
@@ -243,66 +271,76 @@ def tile_selfattentionhybrid_pa_kernel(tc, q, k, x, Wv, bv, out):
             nc.sync.dma_start(out=out_rows[:, c, BANK * h : BANK * (h + 1)], in_=dst)
 
         constants()
-        load_rows("k", 0, 1)
-        load_rows("k", 1, 1)
-        for c in (2, 4, 6):
+        for c in (0, 2, 4, 6):
             load_rows("k", c, 2)
         load_w(0)
-        load_rows("x", 0, 2)
-        load_rows("x", 2, 2)
-        load_w(1)
-        load_rows("x", 4, 2)
-        load_rows("x", 6, 2)
-        for c in (0, 2, 4, 6):
+        for c in (0, 2):
             load_rows("q", c, 2)
-
+        load_w(1)
+        for c in (0, 2, 4, 6):
+            load_rows("x", c, 2)
+        for c in (4, 6):
+            load_rows("q", c, 2)
         for c in range(TILES):
             turn_rows("k", c)
-        for c in range(5):
-            copy_words("k", c, "vector")
-        quantise_rows("k", 0, 0)
-        copy_words("k", 5, "vector")
-        quantise_rows("k", 0, 1)
-        copy_words("k", 6, "vector")
-        copy_words("k", 7, "vector")
-        quantise_rows("k", 1, 0)
-        quantise_rows("k", 1, 1)
-        for g in range(PASSES):
-            regroup_w(g, 0)
-            regroup_w(g, 1)
-            quantise_w(g, 0)
-            quantise_w(g, 1)
-        for c in range(TILES):
-            square_rows("k", c)
+            copy_words("k", c, "vector" if c < 3 else "scalar")
+            if c >= 2:
+                gram("k", c - 2)
+            if c == 4:
+                quantise_rows("k", 0, 0)
+                quantise_rows("k", 0, 1)
+        keep_diagonal("k", 0)
+        regroup_w(0, 0, "vector")
+        turn_rows("q", 0)
+        turn_rows("q", 1)
+        gram("k", 6)
+        turn_rows("q", 2)
+        turn_rows("q", 3)
+        gram("k", 7)
         spread_ksq(0)
-        for c in range(4):
-            turn_rows("x", c)
-        spread_ksq(1)
         spread_bias(0)
         spread_bias(1)
-        for c in range(4, TILES):
-            turn_rows("x", c)
+        quantise_rows("k", 1, 0)
+        quantise_rows("k", 1, 1)
+        regroup_w(0, 1, "vector")
+        keep_diagonal("k", 1)
+        spread_ksq(1)
         for c in range(4):
-            turn_rows("q", c)
-        for c in range(4):
-            copy_words("x", c, "scalar")
+            copy_words("q", c, "scalar")
         copy_ksq(0)
+        square_q(0)
         copy_ksq(1)
-        for c in range(4, TILES):
-            copy_words("x", c, "scalar")
         copy_bias(0)
         copy_bias(1)
-        copy_words("q", 0, "scalar")
-        copy_words("q", 1, "scalar")
-        square_rows("q", 0)
-        copy_words("q", 2, "scalar")
-        copy_words("q", 3, "scalar")
-        square_rows("q", 1)
-        square_rows("q", 2)
-        for half in range(2):
-            for g in range(PASSES):
-                quantise_rows("x", half, g)
-
+        quantise_w(0, 0)
+        quantise_w(0, 1)
+        regroup_w(1, 0, "vector")
+        quantise_rows("q", 0, 0)
+        quantise_rows("q", 0, 1)
+        regroup_w(1, 1, "vector")
+        quantise_w(1, 0)
+        quantise_w(1, 1)
+        for c in range(4):
+            turn_rows("x", c)
+            copy_words("x", c, "scalar")
+        score_matmuls(0, 0)
+        score_matmuls(0, 1)
+        for c in range(4, TILES):
+            turn_rows("x", c)
+            copy_words("x", c, "scalar")
+        score_matmuls(1, 0)
+        score_matmuls(1, 1)
+        for c in range(2):
+            for h in range(2):
+                distance(c, h)
+        first_exp(0)
+        square_q(1)
+        first_exp(1)
+        for c in range(4, TILES):
+            turn_rows("q", c)
+            copy_words("q", c, "scalar")
+        quantise_rows("x", 0, 0)
+        quantise_rows("x", 0, 1)
         v_steps = []
         for n in range(16):
             v_steps.append(("block", n))
@@ -310,12 +348,10 @@ def tile_selfattentionhybrid_pa_kernel(tc, q, k, x, Wv, bv, out):
                 v_steps.append(("words", n // 4 - 1))
         v_steps.append(("words", 3))
         made = [0]
-
         def v_tensor(count):
             for n in range(made[0], min(made[0] + count, 16)):
                 v_matmuls(n)
             made[0] = min(made[0] + count, 16)
-
         def v_vector(blocks):
             while v_steps and (blocks > 0 or len(v_steps) == 1):
                 kind, n = v_steps.pop(0)
@@ -324,67 +360,75 @@ def tile_selfattentionhybrid_pa_kernel(tc, q, k, x, Wv, bv, out):
                     blocks -= 1
                 else:
                     quantise_v(n)
-
-        v_tensor(5 + 2)
-        v_vector(5)
-        quantise_rows("q", 0, 0)
-        quantise_rows("q", 0, 1)
-        score_matmuls(0)
-        score_matmuls(1)
-        distance(0)
-
-        V_BLOCKS = (3, 3, 3, 2)
-        V_DONE = len(V_BLOCKS)
-        OUT_LAG = 3
-        for p in range(TILES):
-            due = [c for c in range(TILES) if max(c + OUT_LAG, V_DONE) == p]
-            blocks = V_BLOCKS[p] if p < V_DONE else 0
-            for c in due:
-                out_matmuls(c)
-            if p == 0:
-                for c in range(4, TILES):
-                    turn_rows("q", c)
-            if p + 2 < TILES:
-                score_matmuls(p + 2)
-            v_tensor(blocks)
-            if p + 1 < TILES:
-                distance(p + 1)
-            first_exp(p)
-            row_max(p)
+        score_matmuls(2, 0)
+        score_matmuls(2, 1)
+        v_tensor(3)
+        score_matmuls(3, 0)
+        score_matmuls(3, 1)
+        row_max(0)
+        quantise_rows("x", 1, 0)
+        quantise_rows("x", 1, 1)
+        distance(2, 0)
+        distance(2, 1)
+        square_q(2)
+        quantise_rows("q", 1, 0)
+        quantise_rows("q", 1, 1)
+        v_vector(1)
+        V_BLOCKS = (3, 3, 3, 3, 3, 0)
+        OUTS = ((), (), (), ((0, 0),), ((1, 0),), ((2, 0),))
+        def engine_of(c, h):
+            return "scalar"
+        for p in range(6):
+            blocks = V_BLOCKS[p]
             if p >= 1:
-                second_exp(p - 1)
                 turn_e(p - 1, 1)
-            if p == 0:
-                for c in range(4, TILES):
-                    copy_words("q", c, "scalar")
-            elif p + 2 < TILES:
-                square_rows("q", p + 2)
-            if p >= 2:
-                copy_e(p - 2, "scalar", 1, 0)
-            if p == 1:
-                quantise_rows("q", 1, 0)
-                quantise_rows("q", 1, 1)
-            v_vector(blocks)
-            for c in due:
-                out_copy(c, 0, "vector")
-                out_copy(c, 1, "vector")
-            if p >= 2:
-                quantise_e(p - 2)
-
-        last = TILES - 1
-        second_exp(last)
-        turn_e(last, 2)
-        out_matmuls(5)
-        copy_e(6, "vector", 1, 0)
+            for c, h in OUTS[p]:
+                out_matmuls(c, h)
+            v_tensor(blocks)
+            if p + 4 < TILES:
+                score_matmuls(p + 4, 0)
+                score_matmuls(p + 4, 1)
+            row_max(p + 1)
+            if p == 5:
+                row_max(7)
+            if p + 3 < TILES:
+                distance(p + 3, 0)
+                distance(p + 3, 1)
+            second_exp(p)
+            if p < 5:
+                first_exp(p + 2)
+            if p + 3 < TILES:
+                square_q(p + 3)
+            if p == 4:
+                first_exp(7)
+            if p >= 1:
+                copy_e(p - 1, "scalar", 1, 0)
+            if p < 5:
+                v_vector(blocks)
+            for c, h in OUTS[p]:
+                out_copy(c, h, engine_of(c, h))
+            if 1 <= p < 5:
+                quantise_e(p - 1)
+        quantise_e(4)
+        second_exp(6)
+        second_exp(7)
+        def outs(l, e):
+            for c, h in l:
+                out_matmuls(c, h)
+            for i, (c, h) in enumerate(l):
+                out_copy(c, h, e[i % len(e)])
+        v_vector(0)
+        turn_e(5, 1)
+        outs(((3, 0), (0, 1)), ["vector"])
+        copy_e(5, "vector", 1, 0)
+        outs(((1, 1), (2, 1)), ["vector"])
+        turn_e(6, 1)
+        turn_e(7, 1)
+        copy_e(6, "scalar", 1, 0)
+        copy_e(7, "scalar", 1, 0)
+        quantise_e(5)
+        outs(((4, 0), (3, 1)), ["vector", "scalar"])
         quantise_e(6)
-        out_matmuls(6)
-        out_copy(5, 0, "scalar")
-        copy_e(last, "scalar", 2, 1)
-        copy_e(last, "vector", 2, 0)
-        quantise_e(last)
-        out_matmuls(last)
-        out_copy(5, 1, "scalar")
-        out_copy(6, 1, "scalar")
-        out_copy(6, 0, "vector")
-        out_copy(last, 0, "vector")
-        out_copy(last, 1, "scalar")
+        quantise_e(7)
+        outs(((4, 1), (5, 0), (5, 1), (6, 0)), ["scalar", "vector"])
+        outs(((6, 1), (7, 0), (7, 1)), ["scalar", "vector"])

@@ -50,12 +50,12 @@ def tile_selfattentionhybrid_pa_kernel(tc, q, k, x, Wv, bv, out):
         warm = const.tile([P, 8], F32, name="warm")
         ident_f = const.tile([P, P], F32, name="ident_f")
         ones_b = const.tile([P, P], BF16, name="ones_b")
-        ones_f = const.tile([P, P], F32, name="ones_f")
-        minus_one = const.tile([P, 1], F32, name="minus_one")
         bias_row = const.tile([P, D], BF16, name="bias_row")
         bias_all = const.tile([P, D], BF16, name="bias_all")
         ksq_all = const.tile([P, S], F32, name="ksq_all")
-        neg_qsq = const.tile([P, TILES * 8], F32, name="neg_qsq")
+        ksq = const.tile([P, TILES, 8], F32, name="ksq")
+        qsq = const.tile([P, TILES, 8], F32, name="qsq")
+        neg_qsq = const.tile([P, TILES, 8], F32, name="neg_qsq")
         words = {}
         scales = {}
         for name in ("k", "q", "x", "w", "v", "e"):
@@ -94,8 +94,6 @@ def tile_selfattentionhybrid_pa_kernel(tc, q, k, x, Wv, bv, out):
             nc.gpsimd.memset(bias_row[:], 0.0)
             nc.gpsimd.dma_start(out=bias_row[0:1, :], in_=bv.unsqueeze(0))
             nc.gpsimd.memset(ones_b[:], 1.0)
-            nc.gpsimd.memset(ones_f[:], 1.0)
-            nc.gpsimd.memset(minus_one[:], -1.0)
 
         def load_rows(name, c, n):
             dst = raw[name][:, D * c : D * (c + n)]
@@ -126,45 +124,23 @@ def tile_selfattentionhybrid_pa_kernel(tc, q, k, x, Wv, bv, out):
             quantise(name, g, slice(BANK * half, BANK * (half + 1)),
                      live[("grouped", name, half)][:, PACK * BANK * g : PACK * BANK * (g + 1)])
 
-        def square_q(c):
+        def square_rows(name, c):
             unused = work.tile([P, D], BF16, name="unused", bufs=1)
-            qsq = small.tile([P, 1], F32, name="qsq")
-            nc.scalar.activation(out=unused[:], in_=raw["q"][:, D * c : D * (c + 1)], func=ACT.Square, accum_out=qsq[:])
-            nc.gpsimd.tensor_scalar(out=neg_qsq[:, 8 * c : 8 * c + 1], in0=qsq[:], scalar1=-1.0, scalar2=0.0, op0=ALU.mult, op1=ALU.add)
-
-        def gram(name, c):
-            half, cc = c // PACK, c % PACK
-            if cc == 0:
-                bank_tile(("gram", name, half), [P, PACK, P], F32)
-            bank = live[("gram", name, half)]
-            features = live[("grouped", name, half)][:].rearrange("p (g c r t) -> p g c r t", g=PASSES, c=PACK, t=PACK)
-            for g in range(PASSES):
-                for t in range(PACK):
-                    operand = features[:, g, cc, :, t]
-                    nc.tensor.matmul(out=bank[:, cc, :], lhsT=operand, rhs=operand, start=g == 0 and t == 0,
-                                     stop=g == PASSES - 1 and t == PACK - 1)
-
-        def keep_diagonal(name, half):
-            live[("diagonal", name, half)] = work.tile([P, PACK, P], F32, name="diagonal", bufs=2)
-            nc.vector.tensor_tensor(out=live[("diagonal", name, half)][:], in0=live[("gram", name, half)][:],
-                                    in1=ident_f[:].unsqueeze(1).to_broadcast([P, PACK, P]), op=ALU.mult)
+            dst = ksq if name == "k" else qsq
+            nc.scalar.activation(out=unused[:], in_=raw[name][:, D * c : D * (c + 1)], func=ACT.Square,
+                                 accum_out=dst[:, c, 0:1])
+            if name == "q":
+                nc.gpsimd.tensor_scalar(out=neg_qsq[:, c, 0:1], in0=qsq[:, c, 0:1], scalar1=-1.0, scalar2=0.0,
+                                        op0=ALU.mult, op1=ALU.add)
 
         def spread_ksq(half):
-            bank = bank_tile(("ksq", half), [P, BANK], F32)
-            nc.tensor.matmul(out=bank[:], lhsT=ones_f[:], rhs=live[("diagonal", "k", half)][:].rearrange("p t r -> p (t r)"),
-                             start=True, stop=True)
-
-        def turn_qsq(half):
-            bank = bank_tile(("qsq", half), [P, PACK], F32)
+            bank = bank_tile(("ksq", half), [P, PACK, P], F32)
             for t in range(PACK):
-                nc.tensor.matmul(out=bank[:, t : t + 1], lhsT=live[("diagonal", "q", half)][:, t, :], rhs=minus_one[:],
+                nc.tensor.matmul(out=bank[:, t, :], lhsT=ksq[:, PACK * half + t, 0:1].to_broadcast([P, P]), rhs=ident_f[:],
                                  start=True, stop=True)
 
-        def copy_qsq(half):
-            nc.scalar.copy(out=neg_qsq[:, 8 * PACK * half : 8 * PACK * (half + 1) : 8], in_=live[("qsq", half)][:])
-
         def copy_ksq(half):
-            nc.scalar.copy(out=ksq_all[:, BANK * half : BANK * (half + 1)], in_=live[("ksq", half)][:])
+            nc.scalar.copy(out=ksq_all[:, BANK * half : BANK * (half + 1)], in_=live[("ksq", half)][:].rearrange("p t r -> p (t r)"))
 
         def spread_bias(half):
             bank = bank_tile(("bias", half), [P, BANK], F32)
@@ -221,7 +197,7 @@ def tile_selfattentionhybrid_pa_kernel(tc, q, k, x, Wv, bv, out):
 
         def first_exp(c):
             sc = live[("scores", c)]
-            nc.scalar.activation(out=sc[:], in_=sc[:], func=ACT.Exp, bias=neg_qsq[:, 8 * c : 8 * c + 1], scale=-1.0)
+            nc.scalar.activation(out=sc[:], in_=sc[:], func=ACT.Exp, bias=neg_qsq[:, c, 0:1], scale=-1.0)
 
         def row_max(c):
             live[("neg_max", c)] = small.tile([P, 1], F32, name="neg_max")
@@ -271,7 +247,9 @@ def tile_selfattentionhybrid_pa_kernel(tc, q, k, x, Wv, bv, out):
             nc.sync.dma_start(out=out_rows[:, c, BANK * h : BANK * (h + 1)], in_=dst)
 
         constants()
-        for c in (0, 2, 4, 6):
+        for c in (0, 1):
+            load_rows("k", c, 1)
+        for c in (2, 4, 6):
             load_rows("k", c, 2)
         load_w(0)
         for c in (0, 2):
@@ -283,40 +261,33 @@ def tile_selfattentionhybrid_pa_kernel(tc, q, k, x, Wv, bv, out):
             load_rows("q", c, 2)
         for c in range(TILES):
             turn_rows("k", c)
-            copy_words("k", c, "vector" if c < 3 else "scalar")
-            if c >= 2:
-                gram("k", c - 2)
+            square_rows("k", c)
+            copy_words("k", c, "vector")
             if c == 4:
                 quantise_rows("k", 0, 0)
+            if c == 5:
                 quantise_rows("k", 0, 1)
-        keep_diagonal("k", 0)
-        regroup_w(0, 0, "vector")
-        turn_rows("q", 0)
-        turn_rows("q", 1)
-        gram("k", 6)
-        turn_rows("q", 2)
-        turn_rows("q", 3)
-        gram("k", 7)
-        spread_ksq(0)
-        spread_bias(0)
-        spread_bias(1)
         quantise_rows("k", 1, 0)
         quantise_rows("k", 1, 1)
-        regroup_w(0, 1, "vector")
-        keep_diagonal("k", 1)
-        spread_ksq(1)
         for c in range(4):
+            turn_rows("q", c)
             copy_words("q", c, "scalar")
+        spread_ksq(0)
+        spread_ksq(1)
+        spread_bias(0)
+        spread_bias(1)
+        square_rows("q", 0)
         copy_ksq(0)
-        square_q(0)
         copy_ksq(1)
         copy_bias(0)
         copy_bias(1)
+        regroup_w(0, 0, "vector")
+        regroup_w(0, 1, "vector")
         quantise_w(0, 0)
         quantise_w(0, 1)
-        regroup_w(1, 0, "vector")
         quantise_rows("q", 0, 0)
         quantise_rows("q", 0, 1)
+        regroup_w(1, 0, "vector")
         regroup_w(1, 1, "vector")
         quantise_w(1, 0)
         quantise_w(1, 1)
@@ -327,14 +298,15 @@ def tile_selfattentionhybrid_pa_kernel(tc, q, k, x, Wv, bv, out):
         score_matmuls(0, 1)
         for c in range(4, TILES):
             turn_rows("x", c)
-            copy_words("x", c, "scalar")
         score_matmuls(1, 0)
         score_matmuls(1, 1)
         for c in range(2):
             for h in range(2):
                 distance(c, h)
         first_exp(0)
-        square_q(1)
+        for c in range(4, TILES):
+            copy_words("x", c, "scalar")
+        square_rows("q", 1)
         first_exp(1)
         for c in range(4, TILES):
             turn_rows("q", c)
@@ -366,13 +338,11 @@ def tile_selfattentionhybrid_pa_kernel(tc, q, k, x, Wv, bv, out):
         score_matmuls(3, 0)
         score_matmuls(3, 1)
         row_max(0)
-        quantise_rows("x", 1, 0)
-        quantise_rows("x", 1, 1)
         distance(2, 0)
         distance(2, 1)
-        square_q(2)
-        quantise_rows("q", 1, 0)
-        quantise_rows("q", 1, 1)
+        square_rows("q", 2)
+        quantise_rows("x", 1, 0)
+        quantise_rows("x", 1, 1)
         v_vector(1)
         V_BLOCKS = (3, 3, 3, 3, 3, 0)
         OUTS = ((), (), (), ((0, 0),), ((1, 0),), ((2, 0),))
@@ -385,20 +355,23 @@ def tile_selfattentionhybrid_pa_kernel(tc, q, k, x, Wv, bv, out):
             for c, h in OUTS[p]:
                 out_matmuls(c, h)
             v_tensor(blocks)
-            if p + 4 < TILES:
-                score_matmuls(p + 4, 0)
-                score_matmuls(p + 4, 1)
             row_max(p + 1)
             if p == 5:
                 row_max(7)
             if p + 3 < TILES:
                 distance(p + 3, 0)
                 distance(p + 3, 1)
+            if p == 0:
+                quantise_rows("q", 1, 0)
+                quantise_rows("q", 1, 1)
+            if p + 4 < TILES:
+                score_matmuls(p + 4, 0)
+                score_matmuls(p + 4, 1)
             second_exp(p)
             if p < 5:
                 first_exp(p + 2)
             if p + 3 < TILES:
-                square_q(p + 3)
+                square_rows("q", p + 3)
             if p == 4:
                 first_exp(7)
             if p >= 1:

@@ -49,8 +49,6 @@ def tile_selfattentionhybrid_pa_kernel(tc, q, k, x, Wv, bv, out):
 
         warm = const.tile([P, 8], F32, name="warm")
         ident_f = const.tile([P, P], F32, name="ident_f")
-        ones_b = const.tile([P, P], BF16, name="ones_b")
-        bias_row = const.tile([P, D], BF16, name="bias_row")
         bias_all = const.tile([P, D], BF16, name="bias_all")
         ksq_all = const.tile([P, S], F32, name="ksq_all")
         ksq = const.tile([P, TILES, 8], F32, name="ksq")
@@ -91,9 +89,6 @@ def tile_selfattentionhybrid_pa_kernel(tc, q, k, x, Wv, bv, out):
             nc.vector.memset(warm[:], 0.0)
             nc.scalar.activation(out=warm[:], in_=warm[:], func=ACT.Exp)
             make_identity(nc, ident_f[:])
-            nc.gpsimd.memset(bias_row[:], 0.0)
-            nc.gpsimd.dma_start(out=bias_row[0:1, :], in_=bv.unsqueeze(0))
-            nc.gpsimd.memset(ones_b[:], 1.0)
 
         def load_rows(name, c, n):
             dst = raw[name][:, D * c : D * (c + n)]
@@ -142,12 +137,8 @@ def tile_selfattentionhybrid_pa_kernel(tc, q, k, x, Wv, bv, out):
         def copy_ksq(half):
             nc.scalar.copy(out=ksq_all[:, BANK * half : BANK * (half + 1)], in_=live[("ksq", half)][:].rearrange("p t r -> p (t r)"))
 
-        def spread_bias(half):
-            bank = bank_tile(("bias", half), [P, BANK], F32)
-            nc.tensor.matmul(out=bank[:], lhsT=ones_b[:], rhs=bias_row[:, BANK * half : BANK * (half + 1)], start=True, stop=True)
-
-        def copy_bias(half):
-            nc.scalar.copy(out=bias_all[:, BANK * half : BANK * (half + 1)], in_=live[("bias", half)][:])
+        def load_bias():
+            nc.sync.dma_start(out=bias_all[:], in_=bv.partition_broadcast(P))
 
         def regroup_w(g, half, engine):
             live[("w", g, half)] = grp.tile([P, PACK * BANK], BF16, name="grp_w", align_bytes=64)
@@ -259,6 +250,7 @@ def tile_selfattentionhybrid_pa_kernel(tc, q, k, x, Wv, bv, out):
             load_rows("x", c, 2)
         for c in (4, 6):
             load_rows("q", c, 2)
+        load_bias()
         for c in range(TILES):
             turn_rows("k", c)
             square_rows("k", c)
@@ -274,13 +266,9 @@ def tile_selfattentionhybrid_pa_kernel(tc, q, k, x, Wv, bv, out):
             copy_words("q", c, "scalar")
         spread_ksq(0)
         spread_ksq(1)
-        spread_bias(0)
-        spread_bias(1)
         square_rows("q", 0)
         copy_ksq(0)
         copy_ksq(1)
-        copy_bias(0)
-        copy_bias(1)
         regroup_w(0, 0, "vector")
         regroup_w(0, 1, "vector")
         quantise_w(0, 0)
@@ -303,11 +291,12 @@ def tile_selfattentionhybrid_pa_kernel(tc, q, k, x, Wv, bv, out):
         for c in range(2):
             for h in range(2):
                 distance(c, h)
+        square_rows("q", 1)
         first_exp(0)
         for c in range(4, TILES):
             copy_words("x", c, "scalar")
-        square_rows("q", 1)
         first_exp(1)
+        square_rows("q", 2)
         for c in range(4, TILES):
             turn_rows("q", c)
             copy_words("q", c, "scalar")
@@ -340,7 +329,7 @@ def tile_selfattentionhybrid_pa_kernel(tc, q, k, x, Wv, bv, out):
         row_max(0)
         distance(2, 0)
         distance(2, 1)
-        square_rows("q", 2)
+        square_rows("q", 3)
         quantise_rows("x", 1, 0)
         quantise_rows("x", 1, 1)
         v_vector(1)
@@ -370,8 +359,8 @@ def tile_selfattentionhybrid_pa_kernel(tc, q, k, x, Wv, bv, out):
             second_exp(p)
             if p < 5:
                 first_exp(p + 2)
-            if p + 3 < TILES:
-                square_rows("q", p + 3)
+            if p + 4 < TILES:
+                square_rows("q", p + 4)
             if p == 4:
                 first_exp(7)
             if p >= 1:

@@ -263,7 +263,7 @@ def tile_selfattentionhybrid_pa_kernel(tc, q, k, x, Wv, bv, out):
         quantise_rows("k", 1, 1)
         for c in range(4):
             turn_rows("q", c)
-            copy_words("q", c, "scalar")
+            copy_words("q", c, "vector" if c < 1 else "scalar")
         spread_ksq(0)
         spread_ksq(1)
         square_rows("q", 0)
@@ -277,20 +277,21 @@ def tile_selfattentionhybrid_pa_kernel(tc, q, k, x, Wv, bv, out):
         quantise_rows("q", 0, 1)
         regroup_w(1, 0, "vector")
         regroup_w(1, 1, "vector")
-        quantise_w(1, 0)
-        quantise_w(1, 1)
         for c in range(4):
             turn_rows("x", c)
-            copy_words("x", c, "scalar")
+            copy_words("x", c, "vector" if c < 0 else "scalar")
         score_matmuls(0, 0)
         score_matmuls(0, 1)
         for c in range(4, TILES):
             turn_rows("x", c)
         score_matmuls(1, 0)
         score_matmuls(1, 1)
-        for c in range(2):
-            for h in range(2):
-                distance(c, h)
+        distance(0, 0)
+        distance(0, 1)
+        quantise_w(1, 0)
+        distance(1, 0)
+        distance(1, 1)
+        quantise_w(1, 1)
         square_rows("q", 1)
         first_exp(0)
         for c in range(4, TILES):
@@ -334,7 +335,7 @@ def tile_selfattentionhybrid_pa_kernel(tc, q, k, x, Wv, bv, out):
         quantise_rows("x", 1, 1)
         v_vector(1)
         V_BLOCKS = (3, 3, 3, 3, 3, 0)
-        OUTS = ((), (), (), ((0, 0),), ((1, 0),), ((2, 0),))
+        OUTS = ((), (), (), ((0, 0),), ((1, 0), (2, 0)), ((3, 0),))
         def engine_of(c, h):
             return "scalar"
         for p in range(6):
@@ -361,14 +362,14 @@ def tile_selfattentionhybrid_pa_kernel(tc, q, k, x, Wv, bv, out):
                 first_exp(p + 2)
             if p + 4 < TILES:
                 square_rows("q", p + 4)
-            if p == 4:
-                first_exp(7)
             if p >= 1:
                 copy_e(p - 1, "scalar", 1, 0)
             if p < 5:
                 v_vector(blocks)
             for c, h in OUTS[p]:
                 out_copy(c, h, engine_of(c, h))
+            if p == 4:
+                first_exp(7)
             if 1 <= p < 5:
                 quantise_e(p - 1)
         quantise_e(4)
@@ -380,16 +381,16 @@ def tile_selfattentionhybrid_pa_kernel(tc, q, k, x, Wv, bv, out):
             for i, (c, h) in enumerate(l):
                 out_copy(c, h, e[i % len(e)])
         v_vector(0)
+        outs(((0, 1), (1, 1)), ["vector"])
         turn_e(5, 1)
-        outs(((3, 0), (0, 1)), ["vector"])
         copy_e(5, "vector", 1, 0)
-        outs(((1, 1), (2, 1)), ["vector"])
+        outs(((2, 1), (3, 1)), ["vector"])
         turn_e(6, 1)
         turn_e(7, 1)
         copy_e(6, "scalar", 1, 0)
         copy_e(7, "scalar", 1, 0)
         quantise_e(5)
-        outs(((4, 0), (3, 1)), ["vector", "scalar"])
+        outs(((4, 0),), ["scalar"])
         quantise_e(6)
         quantise_e(7)
         outs(((4, 1), (5, 0), (5, 1), (6, 0)), ["scalar", "vector"])

@@ -279,7 +279,7 @@ def tile_selfattentionhybrid_pa_kernel(tc, q, k, x, Wv, bv, out):
         regroup_w(1, 1, "vector")
         for c in range(4):
             turn_rows("x", c)
-            copy_words("x", c, "vector" if c < 0 else "scalar")
+            copy_words("x", c, "scalar")
         score_matmuls(0, 0)
         score_matmuls(0, 1)
         for c in range(4, TILES):
@@ -364,34 +364,45 @@ def tile_selfattentionhybrid_pa_kernel(tc, q, k, x, Wv, bv, out):
                 square_rows("q", p + 4)
             if p >= 1:
                 copy_e(p - 1, "scalar", 1, 0)
+            if p == 4:
+                quantise_e(3)
             if p < 5:
                 v_vector(blocks)
             for c, h in OUTS[p]:
                 out_copy(c, h, engine_of(c, h))
             if p == 4:
                 first_exp(7)
-            if 1 <= p < 5:
+            if 1 <= p < 4:
                 quantise_e(p - 1)
-        quantise_e(4)
-        second_exp(6)
-        second_exp(7)
         def outs(l, e):
             for c, h in l:
                 out_matmuls(c, h)
             for i, (c, h) in enumerate(l):
                 out_copy(c, h, e[i % len(e)])
         v_vector(0)
-        outs(((0, 1), (1, 1)), ["vector"])
+        quantise_e(4)
+        out_matmuls(0, 1)
+        out_matmuls(1, 1)
+        out_copy(0, 1, "scalar")
+        second_exp(6)
+        out_copy(1, 1, "scalar")
+        second_exp(7)
+        out_matmuls(2, 1)
         turn_e(5, 1)
+        out_copy(2, 1, "vector")
         copy_e(5, "vector", 1, 0)
-        outs(((2, 1), (3, 1)), ["vector"])
+        out_matmuls(3, 1)
+        out_matmuls(4, 0)
+        out_copy(3, 1, "vector")
         turn_e(6, 1)
+        out_copy(4, 0, "vector")
+        out_matmuls(4, 1)
         turn_e(7, 1)
         copy_e(6, "scalar", 1, 0)
-        copy_e(7, "scalar", 1, 0)
         quantise_e(5)
-        outs(((4, 0),), ["scalar"])
+        out_copy(4, 1, "vector")
+        copy_e(7, "scalar", 1, 0)
         quantise_e(6)
         quantise_e(7)
-        outs(((4, 1), (5, 0), (5, 1), (6, 0)), ["scalar", "vector"])
-        outs(((6, 1), (7, 0), (7, 1)), ["scalar", "vector"])
+        outs(((5, 0), (5, 1), (6, 0), (6, 1)), ["scalar", "vector"])
+        outs(((7, 0), (7, 1)), ["scalar", "vector"])

from contextlib import ExitStack

import concourse.mybir as mybir
from concourse.masks import make_identity

F32 = mybir.dt.float32
BF16 = mybir.dt.bfloat16
U32 = mybir.dt.uint32
U8 = mybir.dt.uint8
FP8X4 = mybir.dt.float8_e4m3fn_x4
ALU = mybir.AluOpType
ACT = mybir.ActivationFunctionType
AX = mybir.AxisListType

P = 128
S = 1024
D = 1024
TILES = S // P
PACK = 4
K_PASS = P * PACK
PASSES = D // K_PASS
BANK = 512
HALVES = S // BANK
FLOPS = 3 * 2 * S * D * D


def tile_selfattentionhybrid_pa_kernel(tc, q, k, x, Wv, bv, out):
    nc = tc.nc
    with ExitStack() as ctx:
        ctx.enter_context(tc.manual_schedule())
        const = ctx.enter_context(tc.tile_pool(name="const", bufs=1))
        raws = ctx.enter_context(tc.tile_pool(name="raws", bufs=1))
        keep = ctx.enter_context(tc.tile_pool(name="keep", bufs=1))
        grp = ctx.enter_context(tc.tile_pool(name="grp", bufs=2))
        work = ctx.enter_context(tc.tile_pool(name="work", bufs=3))
        small = ctx.enter_context(tc.tile_pool(name="small", bufs=4))
        psum = ctx.enter_context(tc.psum_pool(name="psum", bufs=8))

        raw = {}
        for name in ("k", "q", "x", "w"):
            raw[name] = raws.tile([P, TILES * D], BF16, name="raw_" + name)
        rows = {
            "k": k.flatten_outer_dims().rearrange("(c p) f -> p c f", p=P),
            "x": x.flatten_outer_dims().rearrange("(b p e) f -> p b (e f)", p=P, e=2),
            "q": q.flatten_outer_dims().rearrange("(p b e) f -> p b (e f)", p=P, e=2),
        }
        out_rows = out.flatten_outer_dims().rearrange("(p c) d -> p c d", p=P)
        w_rows = Wv.rearrange("(b p e) d -> p b (e d)", b=2 * PASSES, p=P, e=2)

        warm = const.tile([P, 8], F32, name="warm")
        ident_f = const.tile([P, P], F32, name="ident_f")
        bias_all = const.tile([P, D], BF16, name="bias_all")
        ksq_all = const.tile([P, S], F32, name="ksq_all")
        ksq = const.tile([P, TILES, 8], F32, name="ksq")
        qsq = const.tile([P, TILES, 8], F32, name="qsq")
        neg_qsq = const.tile([P, TILES, 8], F32, name="neg_qsq")
        words = {}
        scales = {}
        for name in ("k", "q", "x", "w", "v", "e"):
            words[name] = keep.tile([P, PASSES, S], U32, name="words_" + name, align_bytes=64)
            scales[name] = keep.tile([P, PASSES, S], U8, name="scales_" + name, align_bytes=64)
        e_words = words["e"][:].rearrange("p a (b n) -> p (a b) n", n=PASSES * P)
        e_scales = scales["e"][:].rearrange("p a (b n) -> p (a b) n", n=PASSES * P)
        live = {}

        def bank_tile(key, shape, dtype):
            live[key] = psum.tile(shape, dtype, name="bank", tag="bank")
            return live[key]

        def copy_on(engine, dst, src):
            if engine == "vector":
                nc.vector.tensor_copy(out=dst, in_=src)
            else:
                nc.scalar.copy(out=dst, in_=src)

        def mx_pass(acc, a_words, a_scales, b_words, b_scales, first, last):
            nc.tensor.matmul_mx(out=acc, lhsT=a_words.bitcast(FP8X4), lhsT_scale=a_scales, rhs=b_words.bitcast(FP8X4),
                                rhs_scale=b_scales, start=first, stop=last)

        def mx_group(acc, a, a_cols, b, b_cols):
            for g in range(PASSES):
                mx_pass(acc, words[a][:, g, a_cols], scales[a][:, g, a_cols], words[b][:, g, b_cols],
                        scales[b][:, g, b_cols], g == 0, g == PASSES - 1)

        def quantise(name, g, cols, src):
            nc.vector.quantize_mx(out=words[name][:, g, cols].bitcast(FP8X4), scales=scales[name][:, g, cols], in_=src)

        def constants():
            nc.vector.memset(warm[:], 0.0)
            nc.scalar.activation(out=warm[:], in_=warm[:], func=ACT.Exp)
            make_identity(nc, ident_f[:])

        def load_rows(name, c, n):
            dst = raw[name][:, D * c : D * (c + n)]
            if name == "k":
                nc.sync.dma_start(out=dst.rearrange("p (c f) -> p c f", f=D), in_=rows[name][:, c : c + n, :])
            else:
                nc.sync.dma_start(out=dst, in_=rows[name][:, c // 2, :])

        def load_w(g):
            nc.sync.dma_start(out=raw["w"][:, PACK * D * g : PACK * D * (g + 1)].rearrange("p (b n) -> p b n", b=2),
                              in_=w_rows[:, 2 * g : 2 * g + 2, :])

        def turn_rows(name, c):
            pairs = raw[name][:, D * c : D * (c + 1)].bitcast(F32)
            bank = bank_tile(("turned", name, c), [P, 2 * PASSES, P], F32)
            for b in range(2 * PASSES):
                nc.tensor.transpose(bank[:, b, :], pairs[:, P * b : P * (b + 1)], ident_f[:])

        def copy_words(name, c, engine):
            half, cc = c // PACK, c % PACK
            if ("grouped", name, half) not in live:
                live[("grouped", name, half)] = grp.tile([P, PASSES * PACK * BANK], BF16, name="grp_" + name, tag="grp_t",
                                                         bufs=3, align_bytes=64)
            dst = live[("grouped", name, half)][:].bitcast(F32).rearrange("p (g c r u) -> p g c r u", g=PASSES, c=PACK, u=2)
            copy_on(engine, dst[:, :, cc, :, :], live[("turned", name, c)][:].rearrange("p (g u) r -> p g r u", u=2))

        def quantise_rows(name, half, g):
            quantise(name, g, slice(BANK * half, BANK * (half + 1)),
                     live[("grouped", name, half)][:, PACK * BANK * g : PACK * BANK * (g + 1)])

        def square_rows(name, c):
            unused = work.tile([P, D], BF16, name="unused", bufs=1)
            dst = ksq if name == "k" else qsq
            nc.scalar.activation(out=unused[:], in_=raw[name][:, D * c : D * (c + 1)], func=ACT.Square,
                                 accum_out=dst[:, c, 0:1])
            if name == "q":
                nc.gpsimd.tensor_scalar(out=neg_qsq[:, c, 0:1], in0=qsq[:, c, 0:1], scalar1=-1.0, scalar2=0.0,
                                        op0=ALU.mult, op1=ALU.add)

        def spread_ksq(half):
            bank = bank_tile(("ksq", half), [P, PACK, P], F32)
            for t in range(PACK):
                nc.tensor.matmul(out=bank[:, t, :], lhsT=ksq[:, PACK * half + t, 0:1].to_broadcast([P, P]), rhs=ident_f[:],
                                 start=True, stop=True)

        def copy_ksq(half):
            nc.scalar.copy(out=ksq_all[:, BANK * half : BANK * (half + 1)], in_=live[("ksq", half)][:].rearrange("p t r -> p (t r)"))

        def load_bias():
            nc.sync.dma_start(out=bias_all[:], in_=bv.partition_broadcast(P))

        def regroup_w(g, half, engine):
            live[("w", g, half)] = grp.tile([P, PACK * BANK], BF16, name="grp_w", align_bytes=64)
            src = raw["w"][:, PACK * D * g : PACK * D * (g + 1)].rearrange("p (t d) -> p t d", t=PACK)
            copy_on(engine, live[("w", g, half)][:].rearrange("p (c i t) -> p c t i", i=4, t=PACK),
                    src[:, :, BANK * half : BANK * (half + 1)].rearrange("p t (c i) -> p c t i", i=4))

        def quantise_w(g, half):
            quantise("w", g, slice(BANK * half, BANK * (half + 1)), live[("w", g, half)][:])

        def v_place(n):
            c = 4 * (n // 8) + n % 4
            return (n // 4) % 2, slice(P * c, P * (c + 1))

        def v_matmuls(n):
            kp, cols = v_place(n)
            bank = bank_tile(("v", n), [P, PACK, P], F32)
            for t in range(PACK):
                c = PACK * kp + t
                mx_group(bank[:, t, :], "x", slice(P * c, P * (c + 1)), "w", cols)

        def v_bias(n):
            group = n // 4
            kp, cols = v_place(n)
            if ("v_grouped", group) not in live:
                live[("v_grouped", group)] = grp.tile([P, PACK * BANK], BF16, name="grp_v", align_bytes=64)
            nc.vector.tensor_tensor(
                out=live[("v_grouped", group)][:, BANK * (n % 4) : BANK * (n % 4 + 1)].rearrange("p (d t) -> p d t", t=PACK),
                in0=live[("v", n)][:].rearrange("p t d -> p d t"),
                in1=bias_all[:, cols].unsqueeze(2).to_broadcast([P, P, PACK]),
                op=ALU.add,
            )

        def quantise_v(group):
            quantise("v", group % 2, slice(BANK * (group // 2), BANK * (group // 2 + 1)), live[("v_grouped", group)][:])

        def score_matmuls(c, h):
            mx_group(bank_tile(("qk", c, h), [P, BANK], F32)[:], "q", slice(P * c, P * (c + 1)), "k",
                     slice(BANK * h, BANK * (h + 1)))

        def distance(c, h):
            if h == 0:
                live[("scores", c)] = work.tile([P, S], F32, name="scores", bufs=5)
            cols = slice(BANK * h, BANK * (h + 1))
            nc.vector.scalar_tensor_tensor(out=live[("scores", c)][:, cols], in0=live[("qk", c, h)][:], scalar=-2.0,
                                           in1=ksq_all[:, cols], op0=ALU.mult, op1=ALU.add)

        def first_exp(c):
            sc = live[("scores", c)]
            nc.scalar.activation(out=sc[:], in_=sc[:], func=ACT.Exp, bias=neg_qsq[:, c, 0:1], scale=-1.0)

        def row_max(c):
            live[("neg_max", c)] = small.tile([P, 1], F32, name="neg_max")
            nc.vector.tensor_reduce(out=live[("neg_max", c)][:], in_=live[("scores", c)][:], axis=AX.X, op=ALU.max, negate=True)

        def second_exp(c):
            live[("e", c)] = work.tile([P, S], BF16, name="e")
            live[("row_sum", c)] = small.tile([P, 1], F32, name="row_sum")
            nc.scalar.activation(out=live[("e", c)][:], in_=live[("scores", c)][:], func=ACT.Exp, bias=live[("neg_max", c)][:],
                                 scale=1.0, accum_out=live[("row_sum", c)][:])

        def turn_e(c, banks):
            pairs = live[("e", c)][:].bitcast(F32)
            planes = 2 * PASSES // banks
            for i in range(banks):
                bank = bank_tile(("e_turned", c, i), [P, planes, P], F32)
                for j in range(planes):
                    b = planes * i + j
                    nc.tensor.transpose(bank[:, j, :], pairs[:, P * b : P * (b + 1)], ident_f[:])

        def copy_e(c, engine, banks, i):
            if ("e_grouped", c) not in live:
                live[("e_grouped", c)] = grp.tile([P, S], BF16, name="grp_e", bufs=3, align_bytes=64)
            width = S // banks
            copy_on(engine, live[("e_grouped", c)][:, width * i : width * (i + 1)].bitcast(F32).rearrange("p (g r u) -> p g r u", r=P, u=2),
                    live[("e_turned", c, i)][:].rearrange("p (g u) r -> p g r u", u=2))

        def quantise_e(c):
            nc.vector.quantize_mx(out=e_words[:, c, :].bitcast(FP8X4), scales=e_scales[:, c, :], in_=live[("e_grouped", c)][:])
            live[("inv_sum", c)] = small.tile([P, 1], F32, name="inv_sum", bufs=8)
            nc.vector.reciprocal(out=live[("inv_sum", c)][:], in_=live[("row_sum", c)][:])

        def out_matmuls(c, h):
            bank = bank_tile(("out", c, h), [P, BANK], F32)
            cols = slice(BANK * h, BANK * (h + 1))
            for kp in range(PASSES):
                mx_pass(bank[:], e_words[:, c, P * kp : P * (kp + 1)], e_scales[:, c, P * kp : P * (kp + 1)],
                        words["v"][:, kp, cols], scales["v"][:, kp, cols], kp == 0, kp == PASSES - 1)

        def out_copy(c, h, engine):
            result = work.tile([P, BANK], F32, name="result", bufs=10)
            dst = result[:]
            if engine == "vector":
                nc.vector.tensor_scalar_mul(out=dst, in0=live[("out", c, h)][:], scalar1=live[("inv_sum", c)][:])
            else:
                nc.scalar.activation(out=dst, in_=live[("out", c, h)][:], func=ACT.Copy, scale=live[("inv_sum", c)][:])
            nc.sync.dma_start(out=out_rows[:, c, BANK * h : BANK * (h + 1)], in_=dst)

        constants()
        for c in (0, 1):
            load_rows("k", c, 1)
        for c in (2, 4, 6):
            load_rows("k", c, 2)
        load_w(0)
        for c in (0, 2):
            load_rows("q", c, 2)
        load_w(1)
        for c in (0, 2, 4, 6):
            load_rows("x", c, 2)
        for c in (4, 6):
            load_rows("q", c, 2)
        load_bias()
        for c in range(TILES):
            turn_rows("k", c)
            square_rows("k", c)
            copy_words("k", c, "vector")
            if c == 4:
                quantise_rows("k", 0, 0)
            if c == 5:
                quantise_rows("k", 0, 1)
        quantise_rows("k", 1, 0)
        quantise_rows("k", 1, 1)
        for c in range(4):
            turn_rows("q", c)
            copy_words("q", c, "vector" if c < 1 else "scalar")
        spread_ksq(0)
        spread_ksq(1)
        square_rows("q", 0)
        copy_ksq(0)
        copy_ksq(1)
        regroup_w(0, 0, "vector")
        regroup_w(0, 1, "vector")
        quantise_w(0, 0)
        quantise_w(0, 1)
        quantise_rows("q", 0, 0)
        quantise_rows("q", 0, 1)
        regroup_w(1, 0, "vector")
        regroup_w(1, 1, "vector")
        for c in range(4):
            turn_rows("x", c)
            copy_words("x", c, "scalar")
        score_matmuls(0, 0)
        score_matmuls(0, 1)
        for c in range(4, TILES):
            turn_rows("x", c)
        score_matmuls(1, 0)
        score_matmuls(1, 1)
        distance(0, 0)
        distance(0, 1)
        quantise_w(1, 0)
        distance(1, 0)
        distance(1, 1)
        quantise_w(1, 1)
        square_rows("q", 1)
        first_exp(0)
        for c in range(4, TILES):
            copy_words("x", c, "scalar")
        first_exp(1)
        square_rows("q", 2)
        for c in range(4, TILES):
            turn_rows("q", c)
            copy_words("q", c, "scalar")
        quantise_rows("x", 0, 0)
        quantise_rows("x", 0, 1)
        v_steps = []
        for n in range(16):
            v_steps.append(("block", n))
            if n % 4 == 0 and n > 0:
                v_steps.append(("words", n // 4 - 1))
        v_steps.append(("words", 3))
        made = [0]
        def v_tensor(count):
            for n in range(made[0], min(made[0] + count, 16)):
                v_matmuls(n)
            made[0] = min(made[0] + count, 16)
        def v_vector(blocks):
            while v_steps and (blocks > 0 or len(v_steps) == 1):
                kind, n = v_steps.pop(0)
                if kind == "block":
                    v_bias(n)
                    blocks -= 1
                else:
                    quantise_v(n)
        score_matmuls(2, 0)
        score_matmuls(2, 1)
        v_tensor(3)
        score_matmuls(3, 0)
        score_matmuls(3, 1)
        row_max(0)
        distance(2, 0)
        distance(2, 1)
        square_rows("q", 3)
        quantise_rows("x", 1, 0)
        quantise_rows("x", 1, 1)
        v_vector(1)
        V_BLOCKS = (3, 3, 3, 3, 3, 0)
        OUTS = ((), (), (), ((0, 0),), ((1, 0), (2, 0)), ((3, 0),))
        def engine_of(c, h):
            return "scalar"
        for p in range(6):
            blocks = V_BLOCKS[p]
            if p >= 1:
                turn_e(p - 1, 1)
            for c, h in OUTS[p]:
                out_matmuls(c, h)
            v_tensor(blocks)
            row_max(p + 1)
            if p == 5:
                row_max(7)
            if p + 3 < TILES:
                distance(p + 3, 0)
                distance(p + 3, 1)
            if p == 0:
                quantise_rows("q", 1, 0)
                quantise_rows("q", 1, 1)
            if p + 4 < TILES:
                score_matmuls(p + 4, 0)
                score_matmuls(p + 4, 1)
            second_exp(p)
            if p < 5:
                first_exp(p + 2)
            if p + 4 < TILES:
                square_rows("q", p + 4)
            if p >= 1:
                copy_e(p - 1, "scalar", 1, 0)
            if p == 4:
                quantise_e(3)
            if p < 5:
                v_vector(blocks)
            for c, h in OUTS[p]:
                out_copy(c, h, engine_of(c, h))
            if p == 4:
                first_exp(7)
            if 1 <= p < 4:
                quantise_e(p - 1)
        def outs(l, e):
            for c, h in l:
                out_matmuls(c, h)
            for i, (c, h) in enumerate(l):
                out_copy(c, h, e[i % len(e)])
        v_vector(0)
        quantise_e(4)
        out_matmuls(0, 1)
        out_matmuls(1, 1)
        out_copy(0, 1, "scalar")
        second_exp(6)
        out_copy(1, 1, "scalar")
        second_exp(7)
        out_matmuls(2, 1)
        turn_e(5, 1)
        out_copy(2, 1, "vector")
        copy_e(5, "vector", 1, 0)
        out_matmuls(3, 1)
        out_matmuls(4, 0)
        out_copy(3, 1, "vector")
        turn_e(6, 1)
        out_copy(4, 0, "vector")
        out_matmuls(4, 1)
        turn_e(7, 1)
        copy_e(6, "scalar", 1, 0)
        quantise_e(5)
        out_copy(4, 1, "vector")
        copy_e(7, "scalar", 1, 0)
        quantise_e(6)
        quantise_e(7)
        outs(((5, 0), (5, 1), (6, 0), (6, 1)), ["scalar", "vector"])
        outs(((7, 0), (7, 1)), ["scalar", "vector"])
